import numpy as np
import ml_dtypes


def mxq(x, axis, fmt="e4m3"):
    dtype, down = {"e4m3": (ml_dtypes.float8_e4m3fn, 7), "e5m2": (ml_dtypes.float8_e5m2, 14)}[fmt]
    v = np.moveaxis(np.asarray(x, np.float32).astype(ml_dtypes.bfloat16).astype(np.float64), axis, -1)
    blocks = v.reshape(v.shape[:-1] + (-1, 32))
    amax = np.abs(blocks).max(-1, keepdims=True)
    byte = np.maximum(np.where(amax > 0, np.frexp(amax)[1] - 1 + 127, 0) - down, 1)
    scale = np.exp2(byte - 127.0)
    codes = (blocks / scale).astype(np.float32).astype(dtype).astype(np.float64)
    return np.moveaxis((codes * scale).reshape(v.shape), -1, axis)


WIDE = False


def mx_kscale(k):
    if not WIDE:
        return np.ones(k)
    levels = np.array([10, -10, 5, -5, 0])
    a = np.random.permutation(np.resize(levels, k // 512 * 4)).reshape(k // 512, 4)
    idx = np.arange(k)
    return np.exp2(a[idx // 512, idx % 128 // 32])


BF16 = ml_dtypes.bfloat16


def bf(x):
    return np.asarray(x, np.float32).astype(BF16)


def f64(x):
    return np.asarray(x).astype(np.float64)


E2M1 = np.array([0.0, 0.5, 1.0, 1.5, 2.0, 3.0, 4.0, 6.0, -0.0, -0.5, -1.0, -1.5, -2.0, -3.0, -4.0, -6.0])


def pack_weight(w, fmt):
    k, n = w.shape
    w = f64(bf(w)).reshape(k // 32, 32, n)
    amax = np.abs(w).max(1)
    if fmt == "e4m3":
        byte = np.frexp(amax)[1] - 1 + 127 - 7
    else:
        mant, ex = np.frexp(amax / 6.0)
        byte = np.where(mant > 0.5, ex, ex - 1) + 127
    byte = np.clip(np.where(amax > 0, byte, 1), 1, 254)
    scaled = (w * np.exp2(127.0 - byte)[:, None, :]).reshape(k, n).astype(np.float32)
    by_word = np.ascontiguousarray(scaled.reshape(k // 512, 128, 4, n).transpose(0, 1, 3, 2))
    if fmt == "e4m3":
        words = by_word.astype(ml_dtypes.float8_e4m3fn).view(np.uint8)
    else:
        c = by_word.astype(ml_dtypes.float4_e2m1fn).view(np.uint8) & 0xF
        words = c[..., 0::2] | (c[..., 1::2] << 4)
    return np.ascontiguousarray(words), np.ascontiguousarray(byte.astype(np.uint8).reshape(k // 512, 16, n))


def unpack_weight(words, scales, fmt):
    g, p, n, _ = words.shape
    if fmt == "e4m3":
        vals = np.ascontiguousarray(words).view(ml_dtypes.float8_e4m3fn).astype(np.float64)
    else:
        nib = np.empty((g, p, n, 4), np.uint8)
        nib[..., 0::2] = words & 0xF
        nib[..., 1::2] = words >> 4
        vals = E2M1[nib]
    vals = vals * np.repeat(np.exp2(scales.astype(np.float64) - 127.0), 8, axis=1)[..., None]
    return vals.transpose(0, 1, 3, 2).reshape(g * 512, n)


N, RANK, H, W, B = 4, 512, 64, 64, 128
S = H * W
EPS = 1e-5
XS = 0.01


def setup_inputs():
    t = mx_kscale(RANK)
    U = np.random.standard_normal((N, S, RANK)) * 0.5 / np.sqrt(S)
    U[0] = U[0] * t
    x = bf((np.random.standard_normal((B, 1, H, W)) + 0.5) * XS)
    C = np.random.standard_normal((S, RANK)) / np.sqrt(RANK) / t
    C_words, C_scales = pack_weight(np.ascontiguousarray(C.T), "e4m3")
    return {"x": x,
            "U": bf(U),
            "C_words": C_words,
            "C_scales": C_scales,
            "beta": bf(np.random.standard_normal(S) * 0.5),
            "gamma": bf(1.25 + 0.1 * np.random.standard_normal(1)),
            "bn_bias": bf(0.3 + 0.05 * np.random.standard_normal(1))}


def reference(x, U, C_words, C_scales, beta, gamma, bn_bias):
    x = f64(x)
    b = x.shape[0]
    mean = x.mean(axis=(0, 2, 3), keepdims=True)
    var = x.var(axis=(0, 2, 3), keepdims=True)
    xn = (x - mean) * (1.0 / np.sqrt(var + EPS))
    xn = xn * f64(gamma).reshape(1, -1, 1, 1) + f64(bn_bias).reshape(1, -1, 1, 1)
    z = xn.reshape(b, S)
    t = mxq(z, 1, "e4m3") @ mxq(f64(U), 1, "e4m3")
    h = t[0]
    for n in range(1, N):
        h = t[n] * h + h
    out = (mxq(h, 1, "e4m3") @ unpack_weight(C_words, C_scales, "e4m3")) + f64(beta)
    return out.reshape(b, 1, H, W)

@@ -1,0 +1,220 @@
+import concourse.mybir as mybir
+from concourse.masks import make_identity
+
+F32 = mybir.dt.float32
+BF16 = mybir.dt.bfloat16
+I32 = mybir.dt.int32
+U32 = mybir.dt.uint32
+U8 = mybir.dt.uint8
+FP8X4 = mybir.dt.float8_e4m3fn_x4
+ADD = mybir.AluOpType.add
+MULT = mybir.AluOpType.mult
+IDENTITY = mybir.ActivationFunctionType.Identity
+
+P = 128
+PACK = 4
+K_PASS = P * PACK
+FACTORS = 4
+PIXELS = 4096
+RANK = 512
+EPS = 1e-5
+BANK = 512
+
+PIXEL_PASSES = PIXELS // K_PASS
+CHUNK_PASSES = 2
+CHUNKS = PIXEL_PASSES // CHUNK_PASSES
+OUT_BANKS = PIXELS // BANK
+RUN = 4
+
+FLOPS = 2 * P * PIXELS * RANK * FACTORS + 2 * P * RANK * PIXELS
+
+
+def regroup(copy, grouped, raw):
+    copy(
+        out=grouped.rearrange("p (q i) j -> p q j i", i=RUN),
+        in_=raw.rearrange("p j (q i) -> p q j i", i=RUN),
+    )
+
+
+def tile_generator_pa_kernel(tc, x, U, C_words, C_scales, beta, gamma, bn_bias, out):
+    nc = tc.nc
+    x_rows = x.rearrange("b c h w -> b (c h w)")
+    out_rows = out.rearrange("b c h w -> b (c h w)")
+
+    with (
+        tc.tile_pool(name="keep", bufs=1) as keep,
+        tc.tile_pool(name="raw_pool", bufs=5) as raw_pool,
+        tc.tile_pool(name="grouped_pool", bufs=3) as grouped_pool,
+        tc.tile_pool(name="result_pool", bufs=4) as result_pool,
+        tc.psum_pool(name="psum", bufs=8) as psum,
+    ):
+        ident = keep.tile([P, P], F32)
+        make_identity(nc, ident[:])
+        averager = keep.tile([P, P], F32)
+        nc.vector.memset(averager[:], 1.0 / P)
+        one = keep.tile([P, 1], F32)
+        nc.vector.memset(one[:], 1.0)
+        warm = keep.tile([P, 1], F32)
+        nc.scalar.sqrt(warm[:], one[:])
+        c_scales = keep.tile([P, PIXELS], U8, align_bytes=64)
+        nc.vector.memset(c_scales[:].bitcast(I32), 0)
+
+        x_sb = keep.tile([P, PIXELS], BF16)
+        half = PIXELS // 2
+        nc.sync.dma_start(out=x_sb[:, :half], in_=x_rows[:, :half])
+        nc.sync.dma_start(out=x_sb[:, half:], in_=x_rows[:, half:])
+        gamma_all = keep.tile([P, 1], BF16)
+        nc.scalar.dma_start(out=gamma_all[:], in_=gamma.partition_broadcast(P))
+        bias_all = keep.tile([P, 1], BF16)
+        nc.scalar.dma_start(out=bias_all[:], in_=bn_bias.partition_broadcast(P))
+
+        x_words = x_sb[:].bitcast(F32)
+        words_pass = K_PASS // 2
+        xT = []
+        for pair in range(PIXEL_PASSES // 2):
+            xT_pair = psum.tile([P, 2, 2 * P], F32, name="xT%d" % pair, tag="bank")
+            for c in range(2):
+                first = (2 * pair + c) * words_pass
+                for u in range(2):
+                    nc.tensor.transpose(
+                        xT_pair[:, u, c * P : (c + 1) * P],
+                        x_words[:, first + u : first + words_pass : 2],
+                        ident[:],
+                    )
+            xT.append(xT_pair)
+
+        stats = keep.tile([P, PIXELS // BANK, 6], F32)
+        for i in range(PIXELS // BANK):
+            nc.vector.bn_stats(out=stats[:, i, :], in_=x_sb[:, i * BANK : (i + 1) * BANK])
+        row_stats = keep.tile([P, 2], F32)
+        nc.vector.bn_aggr(out=row_stats[:], in_=stats[:].rearrange("p a s -> p (a s)"))
+        mean = psum.tile([P, 2], F32, tag="bank")
+        nc.tensor.matmul(out=mean[:], lhsT=averager[:], rhs=row_stats[:], start=True, stop=True)
+        offset = keep.tile([P, 1], F32)
+        nc.vector.tensor_sub(out=offset[:], in0=row_stats[:, 0:1], in1=mean[:, 0:1])
+        spread = keep.tile([P, 1], F32)
+        nc.vector.scalar_tensor_tensor(
+            out=spread[:], in0=offset[:], scalar=offset[:, 0:1], in1=row_stats[:, 1:2], op0=MULT, op1=ADD
+        )
+        var = psum.tile([P, 1], F32, tag="bank")
+        nc.tensor.matmul(out=var[:], lhsT=averager[:], rhs=spread[:], start=True, stop=True)
+        var_eps = keep.tile([P, 1], F32)
+        nc.vector.tensor_scalar_add(out=var_eps[:], in0=var[:], scalar1=EPS)
+        std = keep.tile([P, 1], F32)
+        nc.scalar.sqrt(std[:], var_eps[:])
+        rstd = keep.tile([P, 1], F32)
+        nc.vector.reciprocal(out=rstd[:], in_=std[:])
+        gain = keep.tile([P, 1], F32)
+        nc.vector.tensor_mul(out=gain[:], in0=rstd[:], in1=gamma_all[:])
+        mean_gain = keep.tile([P, 1], F32)
+        nc.vector.tensor_mul(out=mean_gain[:], in0=mean[:, 0:1], in1=gain[:])
+        shift = keep.tile([P, 1], F32)
+        nc.vector.tensor_sub(out=shift[:], in0=bias_all[:], in1=mean_gain[:])
+
+        z_grouped = keep.tile([P, PIXEL_PASSES * P, PACK], BF16, align_bytes=64)
+        for pair in range(PIXEL_PASSES // 2):
+            nc.scalar.activation(
+                out=z_grouped[:, 2 * pair * P : 2 * (pair + 1) * P, :].rearrange("p m (u e) -> p m u e", e=2),
+                in_=xT[pair][:].bitcast(BF16).rearrange("p u (m e) -> p m u e", e=2),
+                func=IDENTITY,
+                scale=gain[:, 0:1],
+                bias=shift[:, 0:1],
+            )
+        z_codes = keep.tile([P, PIXEL_PASSES, P], U32, align_bytes=64)
+        z_scales = keep.tile([P, PIXEL_PASSES, P], U8, align_bytes=64)
+        nc.vector.quantize_mx(
+            out=z_codes[:].rearrange("p c b -> p (c b)").bitcast(FP8X4),
+            scales=z_scales[:].rearrange("p c b -> p (c b)"),
+            in_=z_grouped[:].rearrange("p m j -> p (m j)"),
+        )
+
+        u_codes = keep.tile([P, FACTORS * PIXEL_PASSES, RANK], U32, align_bytes=64)
+        u_scales = keep.tile([P, FACTORS * PIXEL_PASSES, RANK], U8, align_bytes=64)
+        c_words = keep.tile([P, PIXELS], U32, align_bytes=64)
+        beta_all = keep.tile([P, PIXELS], BF16)
+        t = []
+        for n in range(FACTORS):
+            t_n = psum.tile([P, RANK], F32, name="t%d" % n, tag="bank")
+            t.append(t_n)
+            for chunk in range(CHUNKS):
+                raw = raw_pool.tile([P, CHUNK_PASSES, PACK, RANK], BF16)
+                first_row = chunk * CHUNK_PASSES * K_PASS
+                nc.sync.dma_start(
+                    out=raw[:],
+                    in_=U[n, first_row : first_row + CHUNK_PASSES * K_PASS, :].rearrange(
+                        "(c p j) r -> p c j r", c=CHUNK_PASSES, j=PACK
+                    ),
+                )
+                grouped = grouped_pool.tile([P, CHUNK_PASSES, RANK, PACK], BF16, align_bytes=64)
+                regroup(nc.vector.tensor_copy, grouped[:, 0], raw[:, 0])
+                regroup(nc.scalar.copy, grouped[:, 1], raw[:, 1])
+                first_pass = n * PIXEL_PASSES + chunk * CHUNK_PASSES
+                passes = slice(first_pass, first_pass + CHUNK_PASSES)
+                nc.vector.quantize_mx(
+                    out=u_codes[:, passes, :].rearrange("p c r -> p (c r)").bitcast(FP8X4),
+                    scales=u_scales[:, passes, :].rearrange("p c r -> p (c r)"),
+                    in_=grouped[:].rearrange("p c r j -> p (c r j)"),
+                )
+                for c in range(chunk * CHUNK_PASSES, (chunk + 1) * CHUNK_PASSES):
+                    nc.tensor.matmul_mx(
+                        out=t_n[:],
+                        lhsT=z_codes[:, c, :].bitcast(FP8X4),
+                        lhsT_scale=z_scales[:, c, :],
+                        rhs=u_codes[:, n * PIXEL_PASSES + c, :].bitcast(FP8X4),
+                        rhs_scale=u_scales[:, n * PIXEL_PASSES + c, :],
+                        start=(c == 0),
+                        stop=(c == PIXEL_PASSES - 1),
+                    )
+            if n == 0:
+                nc.sync.dma_start(
+                    out=c_words[:].bitcast(I32),
+                    in_=C_words[0].rearrange("p n t -> p (n t)").bitcast(I32),
+                )
+            if n == 1:
+                for r in range(4):
+                    nc.sync.dma_start(
+                        out=c_scales[r : P : 32, :].bitcast(I32),
+                        in_=C_scales[0, r : 16 : 4, :].bitcast(I32),
+                    )
+                nc.sync.dma_start(out=beta_all[:], in_=beta.partition_broadcast(P))
+
+        def sorted_ranks(t_n):
+            return t_n[:].rearrange("b (q j) -> b j q", j=PACK)
+
+        h = keep.tile([P, PACK, P], F32, name="h0")
+        nc.scalar.copy(out=h[:], in_=sorted_ranks(t[0]))
+        for n in range(1, FACTORS):
+            h_next = keep.tile([P, PACK, P], F32, name="h%d" % n)
+            nc.vector.scalar_tensor_tensor(
+                out=h_next[:], in0=sorted_ranks(t[n]), scalar=1.0, in1=h[:], op0=ADD, op1=MULT
+            )
+            h = h_next
+
+        hT = psum.tile([P, PACK, P], F32, tag="bank")
+        for j in range(PACK):
+            nc.tensor.transpose(hT[:, j, :], h[:, j, :], ident[:])
+        h_grouped = keep.tile([P, P, PACK], BF16, align_bytes=64)
+        nc.vector.tensor_copy(out=h_grouped[:], in_=hT[:].rearrange("q j b -> q b j"))
+        h_codes = keep.tile([P, P], U32, align_bytes=64)
+        h_scales = keep.tile([P, P], U8, align_bytes=64)
+        nc.vector.quantize_mx(
+            out=h_codes[:].bitcast(FP8X4),
+            scales=h_scales[:],
+            in_=h_grouped[:].rearrange("q b j -> q (b j)"),
+        )
+
+        for o in range(OUT_BANKS):
+            cols = slice(o * BANK, (o + 1) * BANK)
+            product = psum.tile([P, BANK], F32, tag="bank")
+            nc.tensor.matmul_mx(
+                out=product[:],
+                lhsT=h_codes[:].bitcast(FP8X4),
+                lhsT_scale=h_scales[:],
+                rhs=c_words[:, cols].bitcast(FP8X4),
+                rhs_scale=c_scales[:, cols],
+                start=True,
+                stop=True,
+            )
+            result = result_pool.tile([P, BANK], F32)
+            nc.vector.tensor_add(out=result[:], in0=product[:], in1=beta_all[:, cols])
+            nc.sync.dma_start(out=out_rows[:, cols], in_=result[:])

@@ -9,11 +9,11 @@ U8 = mybir.dt.uint8
 FP8X4 = mybir.dt.float8_e4m3fn_x4
 ADD = mybir.AluOpType.add
 MULT = mybir.AluOpType.mult
-IDENTITY = mybir.ActivationFunctionType.Identity
 
 P = 128
 PACK = 4
 K_PASS = P * PACK
+WORDS_PASS = K_PASS // 2
 FACTORS = 4
 PIXELS = 4096
 RANK = 512
@@ -21,19 +21,18 @@ EPS = 1e-5
 BANK = 512
 
 PIXEL_PASSES = PIXELS // K_PASS
-CHUNK_PASSES = 2
-CHUNKS = PIXEL_PASSES // CHUNK_PASSES
+U_PASSES = FACTORS * PIXEL_PASSES
+X_PIECES = 4
 OUT_BANKS = PIXELS // BANK
 RUN = 4
 
 FLOPS = 2 * P * PIXELS * RANK * FACTORS + 2 * P * RANK * PIXELS
 
 
-def regroup(copy, grouped, raw):
-    copy(
-        out=grouped.rearrange("p (q i) j -> p q j i", i=RUN),
-        in_=raw.rearrange("p j (q i) -> p q j i", i=RUN),
-    )
+def transpose_words(nc, out, rows, first_word, ident):
+    words = rows.bitcast(F32)
+    for u in range(2):
+        nc.tensor.transpose(out[:, u, :], words[:, first_word + u : first_word + WORDS_PASS : 2], ident)
 
 
 def tile_generator_pa_kernel(tc, x, U, C_words, C_scales, beta, gamma, bn_bias, out):
@@ -43,11 +42,21 @@ def tile_generator_pa_kernel(tc, x, U, C_words, C_scales, beta, gamma, bn_bias, 
 
     with (
         tc.tile_pool(name="keep", bufs=1) as keep,
-        tc.tile_pool(name="raw_pool", bufs=5) as raw_pool,
-        tc.tile_pool(name="grouped_pool", bufs=3) as grouped_pool,
+        tc.tile_pool(name="raw_pool", bufs=10) as raw_pool,
+        tc.tile_pool(name="grouped_pool", bufs=6) as grouped_pool,
         tc.tile_pool(name="result_pool", bufs=4) as result_pool,
         tc.psum_pool(name="psum", bufs=8) as psum,
     ):
+
+        def load_u_pass(s):
+            n, c = divmod(s, PIXEL_PASSES)
+            raw = raw_pool.tile([P, PACK, RANK], BF16, name="raw")
+            nc.sync.dma_start(
+                out=raw[:],
+                in_=U[n, c * K_PASS : (c + 1) * K_PASS, :].rearrange("(p j) r -> p j r", j=PACK),
+            )
+            return raw
+
         ident = keep.tile([P, P], F32)
         make_identity(nc, ident[:])
         averager = keep.tile([P, P], F32)
@@ -59,29 +68,18 @@ def tile_generator_pa_kernel(tc, x, U, C_words, C_scales, beta, gamma, bn_bias, 
         c_scales = keep.tile([P, PIXELS], U8, align_bytes=64)
         nc.vector.memset(c_scales[:].bitcast(I32), 0)
 
-        x_sb = keep.tile([P, PIXELS], BF16)
-        half = PIXELS // 2
-        nc.sync.dma_start(out=x_sb[:, :half], in_=x_rows[:, :half])
-        nc.sync.dma_start(out=x_sb[:, half:], in_=x_rows[:, half:])
         gamma_all = keep.tile([P, 1], BF16)
         nc.scalar.dma_start(out=gamma_all[:], in_=gamma.partition_broadcast(P))
         bias_all = keep.tile([P, 1], BF16)
         nc.scalar.dma_start(out=bias_all[:], in_=bn_bias.partition_broadcast(P))
-
-        x_words = x_sb[:].bitcast(F32)
-        words_pass = K_PASS // 2
-        xT = []
-        for pair in range(PIXEL_PASSES // 2):
-            xT_pair = psum.tile([P, 2, 2 * P], F32, name="xT%d" % pair, tag="bank")
-            for c in range(2):
-                first = (2 * pair + c) * words_pass
-                for u in range(2):
-                    nc.tensor.transpose(
-                        xT_pair[:, u, c * P : (c + 1) * P],
-                        x_words[:, first + u : first + words_pass : 2],
-                        ident[:],
-                    )
-            xT.append(xT_pair)
+        x_sb = keep.tile([P, PIXELS], BF16)
+        piece = PIXELS // X_PIECES
+        raws = []
+        for i in range(X_PIECES):
+            nc.sync.dma_start(
+                out=x_sb[:, i * piece : (i + 1) * piece], in_=x_rows[:, i * piece : (i + 1) * piece]
+            )
+            raws.append(load_u_pass(i))
 
         stats = keep.tile([P, PIXELS // BANK, 6], F32)
         for i in range(PIXELS // BANK):
@@ -111,14 +109,20 @@ def tile_generator_pa_kernel(tc, x, U, C_words, C_scales, beta, gamma, bn_bias, 
         shift = keep.tile([P, 1], F32)
         nc.vector.tensor_sub(out=shift[:], in0=bias_all[:], in1=mean_gain[:])
 
+        z_sb = keep.tile([P, PIXELS], BF16)
+        nc.vector.tensor_scalar(
+            out=z_sb[:], in0=x_sb[:], scalar1=gain[:, 0:1], scalar2=shift[:, 0:1], op0=MULT, op1=ADD
+        )
         z_grouped = keep.tile([P, PIXEL_PASSES * P, PACK], BF16, align_bytes=64)
         for pair in range(PIXEL_PASSES // 2):
-            nc.scalar.activation(
-                out=z_grouped[:, 2 * pair * P : 2 * (pair + 1) * P, :].rearrange("p m (u e) -> p m u e", e=2),
-                in_=xT[pair][:].bitcast(BF16).rearrange("p u (m e) -> p m u e", e=2),
-                func=IDENTITY,
-                scale=gain[:, 0:1],
-                bias=shift[:, 0:1],
+            zT = psum.tile([P, 2, 2 * P], F32, tag="bank")
+            for c in range(2):
+                transpose_words(
+                    nc, zT[:, :, c * P : (c + 1) * P], z_sb[:], (2 * pair + c) * WORDS_PASS, ident[:]
+                )
+            nc.scalar.copy(
+                out=z_grouped[:, 2 * pair * P : 2 * (pair + 1) * P, :].bitcast(F32),
+                in_=zT[:].rearrange("p u m -> p m u"),
             )
         z_codes = keep.tile([P, PIXEL_PASSES, P], U32, align_bytes=64)
         z_scales = keep.tile([P, PIXEL_PASSES, P], U8, align_bytes=64)
@@ -128,86 +132,73 @@ def tile_generator_pa_kernel(tc, x, U, C_words, C_scales, beta, gamma, bn_bias, 
             in_=z_grouped[:].rearrange("p m j -> p (m j)"),
         )
 
-        u_codes = keep.tile([P, FACTORS * PIXEL_PASSES, RANK], U32, align_bytes=64)
-        u_scales = keep.tile([P, FACTORS * PIXEL_PASSES, RANK], U8, align_bytes=64)
-        c_words = keep.tile([P, PIXELS], U32, align_bytes=64)
-        beta_all = keep.tile([P, PIXELS], BF16)
-        t = []
-        for n in range(FACTORS):
-            t_n = psum.tile([P, RANK], F32, name="t%d" % n, tag="bank")
-            t.append(t_n)
-            for chunk in range(CHUNKS):
-                raw = raw_pool.tile([P, CHUNK_PASSES, PACK, RANK], BF16)
-                first_row = chunk * CHUNK_PASSES * K_PASS
-                nc.sync.dma_start(
-                    out=raw[:],
-                    in_=U[n, first_row : first_row + CHUNK_PASSES * K_PASS, :].rearrange(
-                        "(c p j) r -> p c j r", c=CHUNK_PASSES, j=PACK
-                    ),
-                )
-                grouped = grouped_pool.tile([P, CHUNK_PASSES, RANK, PACK], BF16, align_bytes=64)
-                regroup(nc.vector.tensor_copy, grouped[:, 0], raw[:, 0])
-                regroup(nc.scalar.copy, grouped[:, 1], raw[:, 1])
-                first_pass = n * PIXEL_PASSES + chunk * CHUNK_PASSES
-                passes = slice(first_pass, first_pass + CHUNK_PASSES)
-                nc.vector.quantize_mx(
-                    out=u_codes[:, passes, :].rearrange("p c r -> p (c r)").bitcast(FP8X4),
-                    scales=u_scales[:, passes, :].rearrange("p c r -> p (c r)"),
-                    in_=grouped[:].rearrange("p c r j -> p (c r j)"),
-                )
-                for c in range(chunk * CHUNK_PASSES, (chunk + 1) * CHUNK_PASSES):
-                    nc.tensor.matmul_mx(
-                        out=t_n[:],
-                        lhsT=z_codes[:, c, :].bitcast(FP8X4),
-                        lhsT_scale=z_scales[:, c, :],
-                        rhs=u_codes[:, n * PIXEL_PASSES + c, :].bitcast(FP8X4),
-                        rhs_scale=u_scales[:, n * PIXEL_PASSES + c, :],
-                        start=(c == 0),
-                        stop=(c == PIXEL_PASSES - 1),
-                    )
-            if n == 0:
-                nc.sync.dma_start(
-                    out=c_words[:].bitcast(I32),
-                    in_=C_words[0].rearrange("p n t -> p (n t)").bitcast(I32),
-                )
-            if n == 1:
-                for r in range(4):
-                    nc.sync.dma_start(
-                        out=c_scales[r : P : 32, :].bitcast(I32),
-                        in_=C_scales[0, r : 16 : 4, :].bitcast(I32),
-                    )
-                nc.sync.dma_start(out=beta_all[:], in_=beta.partition_broadcast(P))
-
-        def sorted_ranks(t_n):
-            return t_n[:].rearrange("b (q j) -> b j q", j=PACK)
-
-        h = keep.tile([P, PACK, P], F32, name="h0")
-        nc.scalar.copy(out=h[:], in_=sorted_ranks(t[0]))
-        for n in range(1, FACTORS):
-            h_next = keep.tile([P, PACK, P], F32, name="h%d" % n)
-            nc.vector.scalar_tensor_tensor(
-                out=h_next[:], in0=sorted_ranks(t[n]), scalar=1.0, in1=h[:], op0=ADD, op1=MULT
+        u_codes = keep.tile([P, U_PASSES, RANK], U32, align_bytes=64)
+        u_scales = keep.tile([P, U_PASSES, RANK], U8, align_bytes=64)
+        t = [psum.tile([P, RANK], F32, name="t%d" % n, tag="bank") for n in range(FACTORS)]
+        for s in range(U_PASSES):
+            if s >= X_PIECES:
+                raws.append(load_u_pass(s))
+            grouped = grouped_pool.tile([P, RANK, PACK], BF16, align_bytes=64)
+            copy = nc.scalar.copy if (s < X_PIECES or s % 2 == 1) else nc.vector.tensor_copy
+            copy(
+                out=grouped[:].rearrange("p (q i) j -> p q j i", i=RUN),
+                in_=raws[s][:].rearrange("p j (q i) -> p q j i", i=RUN),
             )
-            h = h_next
+            nc.vector.quantize_mx(
+                out=u_codes[:, s, :].bitcast(FP8X4),
+                scales=u_scales[:, s, :],
+                in_=grouped[:].rearrange("p r j -> p (r j)"),
+            )
+            n, c = divmod(s, PIXEL_PASSES)
+            nc.tensor.matmul_mx(
+                out=t[n][:],
+                lhsT=z_codes[:, c, :].bitcast(FP8X4),
+                lhsT_scale=z_scales[:, c, :],
+                rhs=u_codes[:, s, :].bitcast(FP8X4),
+                rhs_scale=u_scales[:, s, :],
+                start=(c == 0),
+                stop=(c == PIXEL_PASSES - 1),
+            )
 
-        hT = psum.tile([P, PACK, P], F32, tag="bank")
-        for j in range(PACK):
-            nc.tensor.transpose(hT[:, j, :], h[:, j, :], ident[:])
+        beta_all = keep.tile([P, PIXELS], BF16)
+        nc.sync.dma_start(out=beta_all[:], in_=beta.partition_broadcast(P))
+        for r in range(4):
+            nc.sync.dma_start(
+                out=c_scales[r : P : 32, :].bitcast(I32), in_=C_scales[0, r : 16 : 4, :].bitcast(I32)
+            )
+        c_words = keep.tile([P, PIXELS], U32, align_bytes=64)
+        nc.sync.dma_start(
+            out=c_words[:].bitcast(I32), in_=C_words[0].rearrange("p n t -> p (n t)").bitcast(I32)
+        )
+
+        partial = keep.tile([P, RANK], F32, name="partial0")
+        nc.scalar.copy(out=partial[:], in_=t[0][:])
+        for n in range(1, FACTORS):
+            last = n == FACTORS - 1
+            product = keep.tile([P, RANK], BF16 if last else F32, name="partial%d" % n)
+            nc.vector.scalar_tensor_tensor(
+                out=product[:], in0=t[n][:], scalar=1.0, in1=partial[:], op0=ADD, op1=MULT
+            )
+            partial = product
+        h_sb = partial
+
+        hT = psum.tile([P, 2, P], F32, tag="bank")
+        transpose_words(nc, hT[:], h_sb[:], 0, ident[:])
         h_grouped = keep.tile([P, P, PACK], BF16, align_bytes=64)
-        nc.vector.tensor_copy(out=h_grouped[:], in_=hT[:].rearrange("q j b -> q b j"))
+        nc.scalar.copy(out=h_grouped[:].bitcast(F32), in_=hT[:].rearrange("p u b -> p b u"))
         h_codes = keep.tile([P, P], U32, align_bytes=64)
         h_scales = keep.tile([P, P], U8, align_bytes=64)
         nc.vector.quantize_mx(
             out=h_codes[:].bitcast(FP8X4),
             scales=h_scales[:],
-            in_=h_grouped[:].rearrange("q b j -> q (b j)"),
+            in_=h_grouped[:].rearrange("p b j -> p (b j)"),
         )
 
         for o in range(OUT_BANKS):
             cols = slice(o * BANK, (o + 1) * BANK)
-            product = psum.tile([P, BANK], F32, tag="bank")
+            hw = psum.tile([P, BANK], F32, tag="bank")
             nc.tensor.matmul_mx(
-                out=product[:],
+                out=hw[:],
                 lhsT=h_codes[:].bitcast(FP8X4),
                 lhsT_scale=h_scales[:],
                 rhs=c_words[:, cols].bitcast(FP8X4),
@@ -216,5 +207,5 @@ def tile_generator_pa_kernel(tc, x, U, C_words, C_scales, beta, gamma, bn_bias, 
                 stop=True,
             )
             result = result_pool.tile([P, BANK], F32)
-            nc.vector.tensor_add(out=result[:], in0=product[:], in1=beta_all[:, cols])
+            nc.vector.tensor_add(out=result[:], in0=hw[:], in1=beta_all[:, cols])
             nc.sync.dma_start(out=out_rows[:, cols], in_=result[:])

@@ -24,6 +24,7 @@ PIXEL_PASSES = PIXELS // K_PASS
 U_PASSES = FACTORS * PIXEL_PASSES
 X_PIECES = 4
 OUT_BANKS = PIXELS // BANK
+LAST_PIECES = 4
 RUN = 4
 
 FLOPS = 2 * P * PIXELS * RANK * FACTORS + 2 * P * RANK * PIXELS
@@ -42,9 +43,9 @@ def tile_generator_pa_kernel(tc, x, U, C_words, C_scales, beta, gamma, bn_bias, 
 
     with (
         tc.tile_pool(name="keep", bufs=1) as keep,
-        tc.tile_pool(name="raw_pool", bufs=10) as raw_pool,
+        tc.tile_pool(name="raw_pool", bufs=8) as raw_pool,
         tc.tile_pool(name="grouped_pool", bufs=6) as grouped_pool,
-        tc.tile_pool(name="result_pool", bufs=4) as result_pool,
+        tc.tile_pool(name="result_pool", bufs=OUT_BANKS) as result_pool,
         tc.psum_pool(name="psum", bufs=8) as psum,
     ):
 
@@ -160,16 +161,17 @@ def tile_generator_pa_kernel(tc, x, U, C_words, C_scales, beta, gamma, bn_bias, 
                 stop=(c == PIXEL_PASSES - 1),
             )
 
-        beta_all = keep.tile([P, PIXELS], BF16)
-        nc.sync.dma_start(out=beta_all[:], in_=beta.partition_broadcast(P))
         for r in range(4):
             nc.sync.dma_start(
                 out=c_scales[r : P : 32, :].bitcast(I32), in_=C_scales[0, r : 16 : 4, :].bitcast(I32)
             )
         c_words = keep.tile([P, PIXELS], U32, align_bytes=64)
-        nc.sync.dma_start(
-            out=c_words[:].bitcast(I32), in_=C_words[0].rearrange("p n t -> p (n t)").bitcast(I32)
-        )
+        beta_all = keep.tile([P, PIXELS], BF16)
+        c_words_hbm = C_words[0].rearrange("p n t -> p (n t)").bitcast(I32)
+        for i in range(LAST_PIECES):
+            part = slice(i * PIXELS // LAST_PIECES, (i + 1) * PIXELS // LAST_PIECES)
+            nc.sync.dma_start(out=c_words[:, part].bitcast(I32), in_=c_words_hbm[:, part])
+            nc.sync.dma_start(out=beta_all[:, part], in_=beta[part].partition_broadcast(P))
 
         partial = keep.tile([P, RANK], F32, name="partial0")
         nc.scalar.copy(out=partial[:], in_=t[0][:])

@@ -9,6 +9,8 @@ U8 = mybir.dt.uint8
 FP8X4 = mybir.dt.float8_e4m3fn_x4
 ADD = mybir.AluOpType.add
 MULT = mybir.AluOpType.mult
+SUB = mybir.AluOpType.subtract
+MAX = mybir.AluOpType.max
 
 P = 128
 PACK = 4
@@ -23,8 +25,15 @@ BANK = 512
 PIXEL_PASSES = PIXELS // K_PASS
 U_PASSES = FACTORS * PIXEL_PASSES
 X_PIECES = 4
+X_LOAD = 14
+Z_STEP = 16
+SHARED = (0, 1, U_PASSES - 1)
+SCALAR_SHARE = (4, 7)
+RAWS = 8
+LAG = 2
 OUT_BANKS = PIXELS // BANK
 LAST_PIECES = 4
+CATCH_UP = 4
 RUN = 4
 
 FLOPS = 2 * P * PIXELS * RANK * FACTORS + 2 * P * RANK * PIXELS
@@ -43,171 +52,293 @@ def tile_generator_pa_kernel(tc, x, U, C_words, C_scales, beta, gamma, bn_bias, 
 
     with (
         tc.tile_pool(name="keep", bufs=1) as keep,
-        tc.tile_pool(name="raw_pool", bufs=8) as raw_pool,
+        tc.tile_pool(name="raw_pool", bufs=RAWS) as raw_pool,
         tc.tile_pool(name="grouped_pool", bufs=6) as grouped_pool,
         tc.tile_pool(name="result_pool", bufs=OUT_BANKS) as result_pool,
         tc.psum_pool(name="psum", bufs=8) as psum,
     ):
-
-        def load_u_pass(s):
-            n, c = divmod(s, PIXEL_PASSES)
-            raw = raw_pool.tile([P, PACK, RANK], BF16, name="raw")
-            nc.sync.dma_start(
-                out=raw[:],
-                in_=U[n, c * K_PASS : (c + 1) * K_PASS, :].rearrange("(p j) r -> p j r", j=PACK),
-            )
-            return raw
-
         ident = keep.tile([P, P], F32)
         make_identity(nc, ident[:])
         averager = keep.tile([P, P], F32)
-        nc.vector.memset(averager[:], 1.0 / P)
+        nc.vector.memset(averager[:], 1.0 / (P * PIXELS))
+        ones_bf = keep.tile([P, 1], BF16)
+        nc.vector.memset(ones_bf[:], 1.0)
         one = keep.tile([P, 1], F32)
         nc.vector.memset(one[:], 1.0)
         warm = keep.tile([P, 1], F32)
         nc.scalar.sqrt(warm[:], one[:])
+        eps = keep.tile([P, 1], F32)
+        nc.vector.tensor_scalar_mul(out=eps[:], in0=one[:], scalar1=EPS)
         c_scales = keep.tile([P, PIXELS], U8, align_bytes=64)
         nc.vector.memset(c_scales[:].bitcast(I32), 0)
-
         gamma_all = keep.tile([P, 1], BF16)
         nc.scalar.dma_start(out=gamma_all[:], in_=gamma.partition_broadcast(P))
         bias_all = keep.tile([P, 1], BF16)
         nc.scalar.dma_start(out=bias_all[:], in_=bn_bias.partition_broadcast(P))
+
         x_sb = keep.tile([P, PIXELS], BF16)
-        piece = PIXELS // X_PIECES
-        raws = []
-        for i in range(X_PIECES):
-            nc.sync.dma_start(
-                out=x_sb[:, i * piece : (i + 1) * piece], in_=x_rows[:, i * piece : (i + 1) * piece]
-            )
-            raws.append(load_u_pass(i))
-
-        stats = keep.tile([P, PIXELS // BANK, 6], F32)
-        for i in range(PIXELS // BANK):
-            nc.vector.bn_stats(out=stats[:, i, :], in_=x_sb[:, i * BANK : (i + 1) * BANK])
-        row_stats = keep.tile([P, 2], F32)
-        nc.vector.bn_aggr(out=row_stats[:], in_=stats[:].rearrange("p a s -> p (a s)"))
-        mean = psum.tile([P, 2], F32, tag="bank")
-        nc.tensor.matmul(out=mean[:], lhsT=averager[:], rhs=row_stats[:], start=True, stop=True)
-        offset = keep.tile([P, 1], F32)
-        nc.vector.tensor_sub(out=offset[:], in0=row_stats[:, 0:1], in1=mean[:, 0:1])
-        spread = keep.tile([P, 1], F32)
-        nc.vector.scalar_tensor_tensor(
-            out=spread[:], in0=offset[:], scalar=offset[:, 0:1], in1=row_stats[:, 1:2], op0=MULT, op1=ADD
-        )
-        var = psum.tile([P, 1], F32, tag="bank")
-        nc.tensor.matmul(out=var[:], lhsT=averager[:], rhs=spread[:], start=True, stop=True)
-        var_eps = keep.tile([P, 1], F32)
-        nc.vector.tensor_scalar_add(out=var_eps[:], in0=var[:], scalar1=EPS)
-        std = keep.tile([P, 1], F32)
-        nc.scalar.sqrt(std[:], var_eps[:])
-        rstd = keep.tile([P, 1], F32)
-        nc.vector.reciprocal(out=rstd[:], in_=std[:])
-        gain = keep.tile([P, 1], F32)
-        nc.vector.tensor_mul(out=gain[:], in0=rstd[:], in1=gamma_all[:])
-        mean_gain = keep.tile([P, 1], F32)
-        nc.vector.tensor_mul(out=mean_gain[:], in0=mean[:, 0:1], in1=gain[:])
-        shift = keep.tile([P, 1], F32)
-        nc.vector.tensor_sub(out=shift[:], in0=bias_all[:], in1=mean_gain[:])
-
         z_sb = keep.tile([P, PIXELS], BF16)
-        nc.vector.tensor_scalar(
-            out=z_sb[:], in0=x_sb[:], scalar1=gain[:, 0:1], scalar2=shift[:, 0:1], op0=MULT, op1=ADD
-        )
         z_grouped = keep.tile([P, PIXEL_PASSES * P, PACK], BF16, align_bytes=64)
-        for pair in range(PIXEL_PASSES // 2):
-            zT = psum.tile([P, 2, 2 * P], F32, tag="bank")
-            for c in range(2):
-                transpose_words(
-                    nc, zT[:, :, c * P : (c + 1) * P], z_sb[:], (2 * pair + c) * WORDS_PASS, ident[:]
-                )
-            nc.scalar.copy(
-                out=z_grouped[:, 2 * pair * P : 2 * (pair + 1) * P, :].bitcast(F32),
-                in_=zT[:].rearrange("p u m -> p m u"),
-            )
         z_codes = keep.tile([P, PIXEL_PASSES, P], U32, align_bytes=64)
         z_scales = keep.tile([P, PIXEL_PASSES, P], U8, align_bytes=64)
-        nc.vector.quantize_mx(
-            out=z_codes[:].rearrange("p c b -> p (c b)").bitcast(FP8X4),
-            scales=z_scales[:].rearrange("p c b -> p (c b)"),
-            in_=z_grouped[:].rearrange("p m j -> p (m j)"),
-        )
-
         u_codes = keep.tile([P, U_PASSES, RANK], U32, align_bytes=64)
         u_scales = keep.tile([P, U_PASSES, RANK], U8, align_bytes=64)
-        t = [psum.tile([P, RANK], F32, name="t%d" % n, tag="bank") for n in range(FACTORS)]
-        for s in range(U_PASSES):
-            if s >= X_PIECES:
-                raws.append(load_u_pass(s))
-            grouped = grouped_pool.tile([P, RANK, PACK], BF16, align_bytes=64)
-            copy = nc.scalar.copy if (s < X_PIECES or s % 2 == 1) else nc.vector.tensor_copy
-            copy(
-                out=grouped[:].rearrange("p (q i) j -> p q j i", i=RUN),
-                in_=raws[s][:].rearrange("p j (q i) -> p q j i", i=RUN),
-            )
-            nc.vector.quantize_mx(
-                out=u_codes[:, s, :].bitcast(FP8X4),
-                scales=u_scales[:, s, :],
-                in_=grouped[:].rearrange("p r j -> p (r j)"),
-            )
-            n, c = divmod(s, PIXEL_PASSES)
-            nc.tensor.matmul_mx(
-                out=t[n][:],
-                lhsT=z_codes[:, c, :].bitcast(FP8X4),
-                lhsT_scale=z_scales[:, c, :],
-                rhs=u_codes[:, s, :].bitcast(FP8X4),
-                rhs_scale=u_scales[:, s, :],
-                start=(c == 0),
-                stop=(c == PIXEL_PASSES - 1),
-            )
-
-        for r in range(4):
-            nc.sync.dma_start(
-                out=c_scales[r : P : 32, :].bitcast(I32), in_=C_scales[0, r : 16 : 4, :].bitcast(I32)
-            )
         c_words = keep.tile([P, PIXELS], U32, align_bytes=64)
         beta_all = keep.tile([P, PIXELS], BF16)
-        c_words_hbm = C_words[0].rearrange("p n t -> p (n t)").bitcast(I32)
-        for i in range(LAST_PIECES):
-            part = slice(i * PIXELS // LAST_PIECES, (i + 1) * PIXELS // LAST_PIECES)
-            nc.sync.dma_start(out=c_words[:, part].bitcast(I32), in_=c_words_hbm[:, part])
-            nc.sync.dma_start(out=beta_all[:, part], in_=beta[part].partition_broadcast(P))
+        parts = keep.tile([P, 2], F32)
+        mean = keep.tile([P, 2], F32)
+        var = keep.tile([P, 1], F32)
+        minus_var = keep.tile([P, 1], F32)
+        std = keep.tile([P, 1], F32)
+        rstd = keep.tile([P, 1], F32)
+        gain = keep.tile([P, 1], F32)
+        loss = keep.tile([P, 1], F32)
+        raws, groups, t, zT, banks = {}, {}, {}, {}, {}
 
-        partial = keep.tile([P, RANK], F32, name="partial0")
-        nc.scalar.copy(out=partial[:], in_=t[0][:])
-        for n in range(1, FACTORS):
-            last = n == FACTORS - 1
-            product = keep.tile([P, RANK], BF16 if last else F32, name="partial%d" % n)
+        def load_x():
+            piece = PIXELS // X_PIECES
+            for i in range(X_PIECES):
+                cols = slice(i * piece, (i + 1) * piece)
+                nc.sync.dma_start(out=x_sb[:, cols], in_=x_rows[:, cols])
+
+        def load_u(s):
+            if s == X_LOAD:
+                load_x()
+            n, c = divmod(s, PIXEL_PASSES)
+            raws[s] = raw_pool.tile([P, PACK, RANK], BF16, name="raw")
+            source = U[n, c * K_PASS : (c + 1) * K_PASS, :].rearrange("(p j) r -> p j r", j=PACK)
+            pieces = 2 if s in SHARED else 1
+            for i in range(pieces):
+                cols = slice(i * RANK // pieces, (i + 1) * RANK // pieces)
+                nc.sync.dma_start(out=raws[s][:, :, cols], in_=source[:, :, cols])
+
+        def regroup(s):
+            groups[s] = grouped_pool.tile([P, RANK, PACK], BF16, align_bytes=64, name="grouped")
+            taken, of = SCALAR_SHARE
+            on_scalar = (s + 1) * taken // of < (s + 2) * taken // of
+            copies = [nc.scalar.copy] if on_scalar else [nc.vector.tensor_copy]
+            if s in SHARED:
+                copies = [nc.scalar.copy, nc.vector.tensor_copy]
+            if s == U_PASSES - 1:
+                copies = [nc.vector.tensor_copy, nc.scalar.copy]
+            for i, copy in enumerate(copies):
+                cols = slice(i * RANK // len(copies), (i + 1) * RANK // len(copies))
+                copy(
+                    out=groups[s][:, cols, :].rearrange("p (q i) j -> p q j i", i=RUN),
+                    in_=raws[s][:, :, cols].rearrange("p j (q i) -> p q j i", i=RUN),
+                )
+
+        def quantise(s):
+            pieces = 2 if s == U_PASSES - 1 else 1
+            for i in range(pieces):
+                cols = slice(i * RANK // pieces, (i + 1) * RANK // pieces)
+                nc.vector.quantize_mx(
+                    out=u_codes[:, s, cols].bitcast(FP8X4),
+                    scales=u_scales[:, s, cols],
+                    in_=groups[s][:, cols, :].rearrange("p r j -> p (r j)"),
+                )
+
+        def pieces_of(n):
+            return 2 if n == FACTORS - 1 else 1
+
+        def multiply(s):
+            n, c = divmod(s, PIXEL_PASSES)
+            for i in range(pieces_of(n)):
+                width = RANK // pieces_of(n)
+                cols = slice(i * width, (i + 1) * width)
+                if c == 0:
+                    t[n, i] = psum.tile([P, width], F32, name="t%d%d" % (n, i), tag="bank")
+                nc.tensor.matmul_mx(
+                    out=t[n, i][:],
+                    lhsT=z_codes[:, c, :].bitcast(FP8X4),
+                    lhsT_scale=z_scales[:, c, :],
+                    rhs=u_codes[:, s, cols].bitcast(FP8X4),
+                    rhs_scale=u_scales[:, s, cols],
+                    start=(c == 0),
+                    stop=(c == PIXEL_PASSES - 1),
+                )
+
+        def gram_x():
+            gram = psum.tile([P, P], F32, name="gram", tag="bank")
+            sums = psum.tile([P, 1], F32, name="sums", tag="bank")
+            for i in range(PIXELS // P):
+                block = x_sb[:, i * P : (i + 1) * P]
+                first, final = i == 0, i == PIXELS // P - 1
+                nc.tensor.matmul(out=gram[:], lhsT=block, rhs=block, start=first, stop=final)
+                nc.tensor.matmul(out=sums[:], lhsT=block, rhs=ones_bf[:], start=first, stop=final)
+            banks["gram"], banks["sums"] = gram, sums
+
+        def average_x():
+            nc.vector.tensor_copy(out=parts[:, 0:1], in_=banks["sums"][:])
+            diagonal = keep.tile([P, P], F32, name="diagonal")
             nc.vector.scalar_tensor_tensor(
-                out=product[:], in0=t[n][:], scalar=1.0, in1=partial[:], op0=ADD, op1=MULT
+                out=diagonal[:], in0=banks["gram"][:], scalar=1.0, in1=ident[:], op0=MULT, op1=MULT,
+                accum_out=parts[:, 1:2],
             )
-            partial = product
-        h_sb = partial
+            moments = psum.tile([P, 2], F32, name="moments", tag="bank")
+            nc.tensor.matmul(out=moments[:], lhsT=averager[:], rhs=parts[:], start=True, stop=True)
+            banks["moments"] = moments
 
-        hT = psum.tile([P, 2, P], F32, tag="bank")
-        transpose_words(nc, hT[:], h_sb[:], 0, ident[:])
-        h_grouped = keep.tile([P, P, PACK], BF16, align_bytes=64)
-        nc.scalar.copy(out=h_grouped[:].bitcast(F32), in_=hT[:].rearrange("p u b -> p b u"))
-        h_codes = keep.tile([P, P], U32, align_bytes=64)
-        h_scales = keep.tile([P, P], U8, align_bytes=64)
-        nc.vector.quantize_mx(
-            out=h_codes[:].bitcast(FP8X4),
-            scales=h_scales[:],
-            in_=h_grouped[:].rearrange("p b j -> p (b j)"),
-        )
+        def take_moments():
+            nc.vector.tensor_copy(out=mean[:], in_=banks["moments"][:])
 
-        for o in range(OUT_BANKS):
-            cols = slice(o * BANK, (o + 1) * BANK)
-            hw = psum.tile([P, BANK], F32, tag="bank")
-            nc.tensor.matmul_mx(
-                out=hw[:],
-                lhsT=h_codes[:].bitcast(FP8X4),
-                lhsT_scale=h_scales[:],
-                rhs=c_words[:, cols].bitcast(FP8X4),
-                rhs_scale=c_scales[:, cols],
-                start=True,
-                stop=True,
+        def negate_variance():
+            nc.vector.scalar_tensor_tensor(
+                out=minus_var[:], in0=mean[:, 0:1], scalar=mean[:, 0:1], in1=mean[:, 1:2], op0=MULT, op1=SUB
             )
-            result = result_pool.tile([P, BANK], F32)
-            nc.vector.tensor_add(out=result[:], in0=hw[:], in1=beta_all[:, cols])
-            nc.sync.dma_start(out=out_rows[:, cols], in_=result[:])
+
+        def variance():
+            nc.vector.tensor_scalar(out=var[:], in0=minus_var[:], scalar1=-1.0, scalar2=0.0, op0=MULT, op1=MAX)
+
+        def deviation():
+            nc.scalar.activation(out=std[:], in_=var[:], func=mybir.ActivationFunctionType.Sqrt, bias=eps[:])
+
+        def inverse():
+            nc.vector.reciprocal(out=rstd[:], in_=std[:])
+
+        def find_gain():
+            nc.vector.tensor_mul(out=gain[:], in0=rstd[:], in1=gamma_all[:])
+
+        def find_loss():
+            nc.vector.scalar_tensor_tensor(
+                out=loss[:], in0=mean[:, 0:1], scalar=gain[:, 0:1], in1=bias_all[:], op0=MULT, op1=SUB
+            )
+
+        def normalise():
+            nc.vector.tensor_scalar(
+                out=z_sb[:], in0=x_sb[:], scalar1=gain[:, 0:1], scalar2=loss[:, 0:1], op0=MULT, op1=SUB
+            )
+
+        def transpose_z():
+            for pair in range(PIXEL_PASSES // 2):
+                zT[pair] = psum.tile([P, 2, 2 * P], F32, name="zT", tag="bank")
+                for c in range(2):
+                    transpose_words(
+                        nc, zT[pair][:, :, c * P : (c + 1) * P], z_sb[:], (2 * pair + c) * WORDS_PASS, ident[:]
+                    )
+
+        def regroup_z(pairs):
+            for pair in pairs:
+                nc.scalar.copy(
+                    out=z_grouped[:, 2 * pair * P : 2 * (pair + 1) * P, :].bitcast(F32),
+                    in_=zT[pair][:].rearrange("p u m -> p m u"),
+                )
+
+        def quantise_z():
+            nc.vector.quantize_mx(
+                out=z_codes[:].rearrange("p c b -> p (c b)").bitcast(FP8X4),
+                scales=z_scales[:].rearrange("p c b -> p (c b)"),
+                in_=z_grouped[:].rearrange("p m j -> p (m j)"),
+            )
+
+        z_work = [
+            [gram_x, average_x],
+            [],
+            [take_moments],
+            [negate_variance],
+            [variance],
+            [deviation],
+            [],
+            [inverse],
+            [find_gain],
+            [find_loss],
+            [normalise],
+            [transpose_z],
+            [lambda: regroup_z((0, 1))],
+            [lambda: regroup_z((2, 3))],
+            [],
+            [],
+            [],
+            [quantise_z],
+        ]
+        z_done = Z_STEP + (len(z_work) - 1) // 2
+
+        partial = {}
+
+        def combine(n):
+            if n == 0:
+                partial[0] = keep.tile([P, RANK], F32, name="partial0")
+                nc.scalar.copy(out=partial[0][:], in_=t[0, 0][:])
+                return
+            last = n == FACTORS - 1
+            partial[n] = keep.tile([P, RANK], BF16 if last else F32, name="partial%d" % n)
+            for i in range(pieces_of(n)):
+                cols = slice(i * RANK // pieces_of(n), (i + 1) * RANK // pieces_of(n))
+                nc.vector.scalar_tensor_tensor(
+                    out=partial[n][:, cols], in0=t[n, i][:], scalar=1.0, in1=partial[n - 1][:, cols],
+                    op0=ADD, op1=MULT,
+                )
+
+        with tc.manual_schedule():
+            for s in range(RAWS):
+                load_u(s)
+            multiplied = combined = 0
+            for s in range(U_PASSES + LAG):
+                if s < U_PASSES:
+                    regroup(s)
+                    if s + RAWS < U_PASSES:
+                        load_u(s + RAWS)
+                beside = 2 * (s - Z_STEP)
+                if 0 <= beside < len(z_work):
+                    for work in z_work[beside]:
+                        work()
+                if s >= LAG:
+                    quantise(s - LAG)
+                if 0 <= beside < len(z_work) - 1:
+                    for work in z_work[beside + 1]:
+                        work()
+                if s > z_done:
+                    for i in range(CATCH_UP):
+                        if multiplied <= s - LAG:
+                            multiply(multiplied)
+                            multiplied += 1
+                    if combined < FACTORS - 1 and multiplied >= (combined + 1) * PIXEL_PASSES + CATCH_UP:
+                        combine(combined)
+                        combined += 1
+            for n in range(combined, FACTORS):
+                while multiplied < (n + 1) * PIXEL_PASSES:
+                    multiply(multiplied)
+                    multiplied += 1
+                combine(n)
+
+            for r in range(4):
+                nc.sync.dma_start(
+                    out=c_scales[r : P : 32, :].bitcast(I32), in_=C_scales[0, r : 16 : 4, :].bitcast(I32)
+                )
+            c_words_hbm = C_words[0].rearrange("p n t -> p (n t)").bitcast(I32)
+            for i in range(LAST_PIECES):
+                part = slice(i * PIXELS // LAST_PIECES, (i + 1) * PIXELS // LAST_PIECES)
+                nc.sync.dma_start(out=c_words[:, part].bitcast(I32), in_=c_words_hbm[:, part])
+                nc.sync.dma_start(out=beta_all[:, part], in_=beta[part].partition_broadcast(P))
+
+            h_sb = partial[FACTORS - 1]
+            hT = psum.tile([P, 2, P], F32, name="hT", tag="bank")
+            transpose_words(nc, hT[:], h_sb[:], 0, ident[:])
+            h_grouped = keep.tile([P, P, PACK], BF16, align_bytes=64)
+            nc.scalar.copy(out=h_grouped[:].bitcast(F32), in_=hT[:].rearrange("p u b -> p b u"))
+            h_codes = keep.tile([P, P], U32, align_bytes=64)
+            h_scales = keep.tile([P, P], U8, align_bytes=64)
+            nc.vector.quantize_mx(
+                out=h_codes[:].bitcast(FP8X4),
+                scales=h_scales[:],
+                in_=h_grouped[:].rearrange("p b j -> p (b j)"),
+            )
+
+            for o in range(OUT_BANKS):
+                hw = psum.tile([P, BANK], F32, name="hw", tag="bank")
+                result = result_pool.tile([P, BANK], F32, name="result")
+                pieces = 2 if o in (0, OUT_BANKS - 1) else 1
+                for i in range(pieces):
+                    part = slice(i * BANK // pieces, (i + 1) * BANK // pieces)
+                    cols = slice(o * BANK + part.start, o * BANK + part.stop)
+                    nc.tensor.matmul_mx(
+                        out=hw[:, part],
+                        lhsT=h_codes[:].bitcast(FP8X4),
+                        lhsT_scale=h_scales[:],
+                        rhs=c_words[:, cols].bitcast(FP8X4),
+                        rhs_scale=c_scales[:, cols],
+                        start=True,
+                        stop=True,
+                    )
+                    nc.vector.tensor_add(out=result[:, part], in0=hw[:, part], in1=beta_all[:, cols])
+                    nc.sync.dma_start(out=out_rows[:, cols], in_=result[:, part])

@@ -28,7 +28,7 @@ X_PIECES = 4
 X_LOAD = 14
 Z_STEP = 16
 SHARED = (0, 1, U_PASSES - 1)
-SCALAR_SHARE = (4, 7)
+SCALAR_SHARE = (1, 2)
 RAWS = 8
 LAG = 2
 OUT_BANKS = PIXELS // BANK

@@ -25,8 +25,8 @@ BANK = 512
 PIXEL_PASSES = PIXELS // K_PASS
 U_PASSES = FACTORS * PIXEL_PASSES
 X_PIECES = 4
-X_LOAD = 14
-Z_STEP = 16
+X_LOAD = 8
+Z_STEP = 10
 SHARED = (0, 1, U_PASSES - 1)
 SCALAR_SHARE = (1, 2)
 RAWS = 8
@@ -327,18 +327,15 @@ def tile_generator_pa_kernel(tc, x, U, C_words, C_scales, beta, gamma, bn_bias, 
             for o in range(OUT_BANKS):
                 hw = psum.tile([P, BANK], F32, name="hw", tag="bank")
                 result = result_pool.tile([P, BANK], F32, name="result")
-                pieces = 2 if o in (0, OUT_BANKS - 1) else 1
-                for i in range(pieces):
-                    part = slice(i * BANK // pieces, (i + 1) * BANK // pieces)
-                    cols = slice(o * BANK + part.start, o * BANK + part.stop)
-                    nc.tensor.matmul_mx(
-                        out=hw[:, part],
-                        lhsT=h_codes[:].bitcast(FP8X4),
-                        lhsT_scale=h_scales[:],
-                        rhs=c_words[:, cols].bitcast(FP8X4),
-                        rhs_scale=c_scales[:, cols],
-                        start=True,
-                        stop=True,
-                    )
-                    nc.vector.tensor_add(out=result[:, part], in0=hw[:, part], in1=beta_all[:, cols])
-                    nc.sync.dma_start(out=out_rows[:, cols], in_=result[:, part])
+                cols = slice(o * BANK, (o + 1) * BANK)
+                nc.tensor.matmul_mx(
+                    out=hw[:],
+                    lhsT=h_codes[:].bitcast(FP8X4),
+                    lhsT_scale=h_scales[:],
+                    rhs=c_words[:, cols].bitcast(FP8X4),
+                    rhs_scale=c_scales[:, cols],
+                    start=True,
+                    stop=True,
+                )
+                nc.vector.tensor_add(out=result[:], in0=hw[:], in1=beta_all[:, cols])
+                nc.sync.dma_start(out=out_rows[:, cols], in_=result[:])

@@ -25,11 +25,11 @@ BANK = 512
 PIXEL_PASSES = PIXELS // K_PASS
 U_PASSES = FACTORS * PIXEL_PASSES
 X_PIECES = 4
-X_LOAD = 8
-Z_STEP = 10
+X_LOAD = 12
+Z_STEP = 14
 SHARED = (0, 1, U_PASSES - 1)
 SCALAR_SHARE = (1, 2)
-RAWS = 8
+RAWS = 10
 LAG = 2
 OUT_BANKS = PIXELS // BANK
 LAST_PIECES = 4
@@ -52,7 +52,7 @@ def tile_generator_pa_kernel(tc, x, U, C_words, C_scales, beta, gamma, bn_bias, 
 
     with (
         tc.tile_pool(name="keep", bufs=1) as keep,
-        tc.tile_pool(name="raw_pool", bufs=RAWS) as raw_pool,
+        tc.tile_pool(name="raw_pool", bufs=RAWS // 2) as raw_pool,
         tc.tile_pool(name="grouped_pool", bufs=6) as grouped_pool,
         tc.tile_pool(name="result_pool", bufs=OUT_BANKS) as result_pool,
         tc.psum_pool(name="psum", bufs=8) as psum,
@@ -105,12 +105,20 @@ def tile_generator_pa_kernel(tc, x, U, C_words, C_scales, beta, gamma, bn_bias, 
             if s == X_LOAD:
                 load_x()
             n, c = divmod(s, PIXEL_PASSES)
-            raws[s] = raw_pool.tile([P, PACK, RANK], BF16, name="raw")
-            source = U[n, c * K_PASS : (c + 1) * K_PASS, :].rearrange("(p j) r -> p j r", j=PACK)
+            if s % 2 == 0:
+                raws[s // 2] = raw_pool.tile([P, 2, PACK, RANK], BF16, name="raw")
+            raw = raws[s // 2]
+            rows = U[n, c * K_PASS : (c + 1) * K_PASS, :]
+            if 2 <= s < U_PASSES - 2:
+                if s % 2 == 0:
+                    rows = U[n, c * K_PASS : (c + 2) * K_PASS, :]
+                    nc.sync.dma_start(out=raw[:], in_=rows.rearrange("(e p j) r -> p e j r", e=2, j=PACK))
+                return
+            source = rows.rearrange("(p j) r -> p j r", j=PACK)
             pieces = 2 if s in SHARED else 1
             for i in range(pieces):
                 cols = slice(i * RANK // pieces, (i + 1) * RANK // pieces)
-                nc.sync.dma_start(out=raws[s][:, :, cols], in_=source[:, :, cols])
+                nc.sync.dma_start(out=raw[:, s % 2, :, cols], in_=source[:, :, cols])
 
         def regroup(s):
             groups[s] = grouped_pool.tile([P, RANK, PACK], BF16, align_bytes=64, name="grouped")
@@ -125,7 +133,7 @@ def tile_generator_pa_kernel(tc, x, U, C_words, C_scales, beta, gamma, bn_bias, 
                 cols = slice(i * RANK // len(copies), (i + 1) * RANK // len(copies))
                 copy(
                     out=groups[s][:, cols, :].rearrange("p (q i) j -> p q j i", i=RUN),
-                    in_=raws[s][:, :, cols].rearrange("p j (q i) -> p q j i", i=RUN),
+                    in_=raws[s // 2][:, s % 2, :, cols].rearrange("p j (q i) -> p q j i", i=RUN),
                 )
 
         def quantise(s):
@@ -276,7 +284,8 @@ def tile_generator_pa_kernel(tc, x, U, C_words, C_scales, beta, gamma, bn_bias, 
             for s in range(U_PASSES + LAG):
                 if s < U_PASSES:
                     regroup(s)
-                    if s + RAWS < U_PASSES:
+                    if s % 2 == 1 and s + RAWS < U_PASSES:
+                        load_u(s + RAWS - 1)
                         load_u(s + RAWS)
                 beside = 2 * (s - Z_STEP)
                 if 0 <= beside < len(z_work):

@@ -34,7 +34,7 @@ LAG = 2
 OUT_BANKS = PIXELS // BANK
 LAST_PIECES = 4
 CATCH_UP = 4
-RUN = 4
+RUN = 2
 
 FLOPS = 2 * P * PIXELS * RANK * FACTORS + 2 * P * RANK * PIXELS
 

@@ -25,16 +25,17 @@ BANK = 512
 PIXEL_PASSES = PIXELS // K_PASS
 U_PASSES = FACTORS * PIXEL_PASSES
 X_PIECES = 4
-X_LOAD = 12
-Z_STEP = 14
+X_LOAD = 14
+Z_STEP = 16
 SHARED = (0, 1, U_PASSES - 1)
 SCALAR_SHARE = (1, 2)
 RAWS = 10
 LAG = 2
 OUT_BANKS = PIXELS // BANK
 LAST_PIECES = 4
+SINGLES = 4
 CATCH_UP = 4
-RUN = 2
+RUN = 4
 
 FLOPS = 2 * P * PIXELS * RANK * FACTORS + 2 * P * RANK * PIXELS
 
@@ -53,7 +54,7 @@ def tile_generator_pa_kernel(tc, x, U, C_words, C_scales, beta, gamma, bn_bias, 
     with (
         tc.tile_pool(name="keep", bufs=1) as keep,
         tc.tile_pool(name="raw_pool", bufs=RAWS // 2) as raw_pool,
-        tc.tile_pool(name="grouped_pool", bufs=6) as grouped_pool,
+        tc.tile_pool(name="grouped_pool", bufs=4) as grouped_pool,
         tc.tile_pool(name="result_pool", bufs=OUT_BANKS) as result_pool,
         tc.psum_pool(name="psum", bufs=8) as psum,
     ):
@@ -109,7 +110,7 @@ def tile_generator_pa_kernel(tc, x, U, C_words, C_scales, beta, gamma, bn_bias, 
                 raws[s // 2] = raw_pool.tile([P, 2, PACK, RANK], BF16, name="raw")
             raw = raws[s // 2]
             rows = U[n, c * K_PASS : (c + 1) * K_PASS, :]
-            if 2 <= s < U_PASSES - 2:
+            if SINGLES <= s < U_PASSES - 2:
                 if s % 2 == 0:
                     rows = U[n, c * K_PASS : (c + 2) * K_PASS, :]
                     nc.sync.dma_start(out=raw[:], in_=rows.rearrange("(e p j) r -> p e j r", e=2, j=PACK))
@@ -121,7 +122,9 @@ def tile_generator_pa_kernel(tc, x, U, C_words, C_scales, beta, gamma, bn_bias, 
                 nc.sync.dma_start(out=raw[:, s % 2, :, cols], in_=source[:, :, cols])
 
         def regroup(s):
-            groups[s] = grouped_pool.tile([P, RANK, PACK], BF16, align_bytes=64, name="grouped")
+            if s % 2 == 0:
+                groups[s // 2] = grouped_pool.tile([P, 2, RANK, PACK], BF16, align_bytes=64, name="grouped")
+            grouped = groups[s // 2][:, s % 2, :, :]
             taken, of = SCALAR_SHARE
             on_scalar = (s + 1) * taken // of < (s + 2) * taken // of
             copies = [nc.scalar.copy] if on_scalar else [nc.vector.tensor_copy]
@@ -132,18 +135,26 @@ def tile_generator_pa_kernel(tc, x, U, C_words, C_scales, beta, gamma, bn_bias, 
             for i, copy in enumerate(copies):
                 cols = slice(i * RANK // len(copies), (i + 1) * RANK // len(copies))
                 copy(
-                    out=groups[s][:, cols, :].rearrange("p (q i) j -> p q j i", i=RUN),
+                    out=grouped[:, cols, :].rearrange("p (q i) j -> p q j i", i=RUN),
                     in_=raws[s // 2][:, s % 2, :, cols].rearrange("p j (q i) -> p q j i", i=RUN),
                 )
 
         def quantise(s):
+            if 2 <= s < U_PASSES - 2:
+                if s % 2 == 1:
+                    nc.vector.quantize_mx(
+                        out=u_codes[:, s - 1 : s + 1, :].rearrange("p e r -> p (e r)").bitcast(FP8X4),
+                        scales=u_scales[:, s - 1 : s + 1, :].rearrange("p e r -> p (e r)"),
+                        in_=groups[s // 2][:].rearrange("p e r j -> p (e r j)"),
+                    )
+                return
             pieces = 2 if s == U_PASSES - 1 else 1
             for i in range(pieces):
                 cols = slice(i * RANK // pieces, (i + 1) * RANK // pieces)
                 nc.vector.quantize_mx(
                     out=u_codes[:, s, cols].bitcast(FP8X4),
                     scales=u_scales[:, s, cols],
-                    in_=groups[s][:, cols, :].rearrange("p r j -> p (r j)"),
+                    in_=groups[s // 2][:, s % 2, cols, :].rearrange("p r j -> p (r j)"),
                 )
 
         def pieces_of(n):

import concourse.mybir as mybir
from concourse.masks import make_identity

F32 = mybir.dt.float32
BF16 = mybir.dt.bfloat16
I32 = mybir.dt.int32
U32 = mybir.dt.uint32
U8 = mybir.dt.uint8
FP8X4 = mybir.dt.float8_e4m3fn_x4
ADD = mybir.AluOpType.add
MULT = mybir.AluOpType.mult
SUB = mybir.AluOpType.subtract
MAX = mybir.AluOpType.max

P = 128
PACK = 4
K_PASS = P * PACK
WORDS_PASS = K_PASS // 2
FACTORS = 4
PIXELS = 4096
RANK = 512
EPS = 1e-5
BANK = 512

PIXEL_PASSES = PIXELS // K_PASS
U_PASSES = FACTORS * PIXEL_PASSES
X_PIECES = 4
X_LOAD = 14
Z_STEP = 16
SHARED = (0, 1, U_PASSES - 1)
SCALAR_SHARE = (1, 2)
RAWS = 10
LAG = 2
OUT_BANKS = PIXELS // BANK
LAST_PIECES = 4
SINGLES = 4
CATCH_UP = 4
RUN = 4

FLOPS = 2 * P * PIXELS * RANK * FACTORS + 2 * P * RANK * PIXELS


def transpose_words(nc, out, rows, first_word, ident):
    words = rows.bitcast(F32)
    for u in range(2):
        nc.tensor.transpose(out[:, u, :], words[:, first_word + u : first_word + WORDS_PASS : 2], ident)


def tile_generator_pa_kernel(tc, x, U, C_words, C_scales, beta, gamma, bn_bias, out):
    nc = tc.nc
    x_rows = x.rearrange("b c h w -> b (c h w)")
    out_rows = out.rearrange("b c h w -> b (c h w)")

    with (
        tc.tile_pool(name="keep", bufs=1) as keep,
        tc.tile_pool(name="raw_pool", bufs=RAWS // 2) as raw_pool,
        tc.tile_pool(name="grouped_pool", bufs=4) as grouped_pool,
        tc.tile_pool(name="result_pool", bufs=OUT_BANKS) as result_pool,
        tc.psum_pool(name="psum", bufs=8) as psum,
    ):
        ident = keep.tile([P, P], F32)
        make_identity(nc, ident[:])
        averager = keep.tile([P, P], F32)
        nc.vector.memset(averager[:], 1.0 / (P * PIXELS))
        ones_bf = keep.tile([P, 1], BF16)
        nc.vector.memset(ones_bf[:], 1.0)
        one = keep.tile([P, 1], F32)
        nc.vector.memset(one[:], 1.0)
        warm = keep.tile([P, 1], F32)
        nc.scalar.sqrt(warm[:], one[:])
        eps = keep.tile([P, 1], F32)
        nc.vector.tensor_scalar_mul(out=eps[:], in0=one[:], scalar1=EPS)
        c_scales = keep.tile([P, PIXELS], U8, align_bytes=64)
        nc.vector.memset(c_scales[:].bitcast(I32), 0)
        gamma_all = keep.tile([P, 1], BF16)
        nc.scalar.dma_start(out=gamma_all[:], in_=gamma.partition_broadcast(P))
        bias_all = keep.tile([P, 1], BF16)
        nc.scalar.dma_start(out=bias_all[:], in_=bn_bias.partition_broadcast(P))

        x_sb = keep.tile([P, PIXELS], BF16)
        z_sb = keep.tile([P, PIXELS], BF16)
        z_grouped = keep.tile([P, PIXEL_PASSES * P, PACK], BF16, align_bytes=64)
        z_codes = keep.tile([P, PIXEL_PASSES, P], U32, align_bytes=64)
        z_scales = keep.tile([P, PIXEL_PASSES, P], U8, align_bytes=64)
        u_codes = keep.tile([P, U_PASSES, RANK], U32, align_bytes=64)
        u_scales = keep.tile([P, U_PASSES, RANK], U8, align_bytes=64)
        c_words = keep.tile([P, PIXELS], U32, align_bytes=64)
        beta_all = keep.tile([P, PIXELS], BF16)
        parts = keep.tile([P, 2], F32)
        mean = keep.tile([P, 2], F32)
        var = keep.tile([P, 1], F32)
        minus_var = keep.tile([P, 1], F32)
        std = keep.tile([P, 1], F32)
        rstd = keep.tile([P, 1], F32)
        gain = keep.tile([P, 1], F32)
        loss = keep.tile([P, 1], F32)
        raws, groups, t, zT, banks = {}, {}, {}, {}, {}

        def load_x():
            piece = PIXELS // X_PIECES
            for i in range(X_PIECES):
                cols = slice(i * piece, (i + 1) * piece)
                nc.sync.dma_start(out=x_sb[:, cols], in_=x_rows[:, cols])

        def load_u(s):
            if s == X_LOAD:
                load_x()
            n, c = divmod(s, PIXEL_PASSES)
            if s % 2 == 0:
                raws[s // 2] = raw_pool.tile([P, 2, PACK, RANK], BF16, name="raw")
            raw = raws[s // 2]
            rows = U[n, c * K_PASS : (c + 1) * K_PASS, :]
            if SINGLES <= s < U_PASSES - 2:
                if s % 2 == 0:
                    rows = U[n, c * K_PASS : (c + 2) * K_PASS, :]
                    nc.sync.dma_start(out=raw[:], in_=rows.rearrange("(e p j) r -> p e j r", e=2, j=PACK))
                return
            source = rows.rearrange("(p j) r -> p j r", j=PACK)
            pieces = 2 if s in SHARED else 1
            for i in range(pieces):
                cols = slice(i * RANK // pieces, (i + 1) * RANK // pieces)
                nc.sync.dma_start(out=raw[:, s % 2, :, cols], in_=source[:, :, cols])

        def regroup(s):
            if s % 2 == 0:
                groups[s // 2] = grouped_pool.tile([P, 2, RANK, PACK], BF16, align_bytes=64, name="grouped")
            grouped = groups[s // 2][:, s % 2, :, :]
            taken, of = SCALAR_SHARE
            on_scalar = (s + 1) * taken // of < (s + 2) * taken // of
            copies = [nc.scalar.copy] if on_scalar else [nc.vector.tensor_copy]
            if s in SHARED:
                copies = [nc.scalar.copy, nc.vector.tensor_copy]
            if s == U_PASSES - 1:
                copies = [nc.vector.tensor_copy, nc.scalar.copy]
            for i, copy in enumerate(copies):
                cols = slice(i * RANK // len(copies), (i + 1) * RANK // len(copies))
                copy(
                    out=grouped[:, cols, :].rearrange("p (q i) j -> p q j i", i=RUN),
                    in_=raws[s // 2][:, s % 2, :, cols].rearrange("p j (q i) -> p q j i", i=RUN),
                )

        def quantise(s):
            if 2 <= s < U_PASSES - 2:
                if s % 2 == 1:
                    nc.vector.quantize_mx(
                        out=u_codes[:, s - 1 : s + 1, :].rearrange("p e r -> p (e r)").bitcast(FP8X4),
                        scales=u_scales[:, s - 1 : s + 1, :].rearrange("p e r -> p (e r)"),
                        in_=groups[s // 2][:].rearrange("p e r j -> p (e r j)"),
                    )
                return
            pieces = 2 if s == U_PASSES - 1 else 1
            for i in range(pieces):
                cols = slice(i * RANK // pieces, (i + 1) * RANK // pieces)
                nc.vector.quantize_mx(
                    out=u_codes[:, s, cols].bitcast(FP8X4),
                    scales=u_scales[:, s, cols],
                    in_=groups[s // 2][:, s % 2, cols, :].rearrange("p r j -> p (r j)"),
                )

        def pieces_of(n):
            return 2 if n == FACTORS - 1 else 1

        def multiply(s):
            n, c = divmod(s, PIXEL_PASSES)
            for i in range(pieces_of(n)):
                width = RANK // pieces_of(n)
                cols = slice(i * width, (i + 1) * width)
                if c == 0:
                    t[n, i] = psum.tile([P, width], F32, name="t%d%d" % (n, i), tag="bank")
                nc.tensor.matmul_mx(
                    out=t[n, i][:],
                    lhsT=z_codes[:, c, :].bitcast(FP8X4),
                    lhsT_scale=z_scales[:, c, :],
                    rhs=u_codes[:, s, cols].bitcast(FP8X4),
                    rhs_scale=u_scales[:, s, cols],
                    start=(c == 0),
                    stop=(c == PIXEL_PASSES - 1),
                )

        def gram_x():
            gram = psum.tile([P, P], F32, name="gram", tag="bank")
            sums = psum.tile([P, 1], F32, name="sums", tag="bank")
            for i in range(PIXELS // P):
                block = x_sb[:, i * P : (i + 1) * P]
                first, final = i == 0, i == PIXELS // P - 1
                nc.tensor.matmul(out=gram[:], lhsT=block, rhs=block, start=first, stop=final)
                nc.tensor.matmul(out=sums[:], lhsT=block, rhs=ones_bf[:], start=first, stop=final)
            banks["gram"], banks["sums"] = gram, sums

        def average_x():
            nc.vector.tensor_copy(out=parts[:, 0:1], in_=banks["sums"][:])
            diagonal = keep.tile([P, P], F32, name="diagonal")
            nc.vector.scalar_tensor_tensor(
                out=diagonal[:], in0=banks["gram"][:], scalar=1.0, in1=ident[:], op0=MULT, op1=MULT,
                accum_out=parts[:, 1:2],
            )
            moments = psum.tile([P, 2], F32, name="moments", tag="bank")
            nc.tensor.matmul(out=moments[:], lhsT=averager[:], rhs=parts[:], start=True, stop=True)
            banks["moments"] = moments

        def take_moments():
            nc.vector.tensor_copy(out=mean[:], in_=banks["moments"][:])

        def negate_variance():
            nc.vector.scalar_tensor_tensor(
                out=minus_var[:], in0=mean[:, 0:1], scalar=mean[:, 0:1], in1=mean[:, 1:2], op0=MULT, op1=SUB
            )

        def variance():
            nc.vector.tensor_scalar(out=var[:], in0=minus_var[:], scalar1=-1.0, scalar2=0.0, op0=MULT, op1=MAX)

        def deviation():
            nc.scalar.activation(out=std[:], in_=var[:], func=mybir.ActivationFunctionType.Sqrt, bias=eps[:])

        def inverse():
            nc.vector.reciprocal(out=rstd[:], in_=std[:])

        def find_gain():
            nc.vector.tensor_mul(out=gain[:], in0=rstd[:], in1=gamma_all[:])

        def find_loss():
            nc.vector.scalar_tensor_tensor(
                out=loss[:], in0=mean[:, 0:1], scalar=gain[:, 0:1], in1=bias_all[:], op0=MULT, op1=SUB
            )

        def normalise():
            nc.vector.tensor_scalar(
                out=z_sb[:], in0=x_sb[:], scalar1=gain[:, 0:1], scalar2=loss[:, 0:1], op0=MULT, op1=SUB
            )

        def transpose_z():
            for pair in range(PIXEL_PASSES // 2):
                zT[pair] = psum.tile([P, 2, 2 * P], F32, name="zT", tag="bank")
                for c in range(2):
                    transpose_words(
                        nc, zT[pair][:, :, c * P : (c + 1) * P], z_sb[:], (2 * pair + c) * WORDS_PASS, ident[:]
                    )

        def regroup_z(pairs):
            for pair in pairs:
                nc.scalar.copy(
                    out=z_grouped[:, 2 * pair * P : 2 * (pair + 1) * P, :].bitcast(F32),
                    in_=zT[pair][:].rearrange("p u m -> p m u"),
                )

        def quantise_z():
            nc.vector.quantize_mx(
                out=z_codes[:].rearrange("p c b -> p (c b)").bitcast(FP8X4),
                scales=z_scales[:].rearrange("p c b -> p (c b)"),
                in_=z_grouped[:].rearrange("p m j -> p (m j)"),
            )

        z_work = [
            [gram_x, average_x],
            [],
            [take_moments],
            [negate_variance],
            [variance],
            [deviation],
            [],
            [inverse],
            [find_gain],
            [find_loss],
            [normalise],
            [transpose_z],
            [lambda: regroup_z((0, 1))],
            [lambda: regroup_z((2, 3))],
            [],
            [],
            [],
            [quantise_z],
        ]
        z_done = Z_STEP + (len(z_work) - 1) // 2

        partial = {}

        def combine(n):
            if n == 0:
                partial[0] = keep.tile([P, RANK], F32, name="partial0")
                nc.scalar.copy(out=partial[0][:], in_=t[0, 0][:])
                return
            last = n == FACTORS - 1
            partial[n] = keep.tile([P, RANK], BF16 if last else F32, name="partial%d" % n)
            for i in range(pieces_of(n)):
                cols = slice(i * RANK // pieces_of(n), (i + 1) * RANK // pieces_of(n))
                nc.vector.scalar_tensor_tensor(
                    out=partial[n][:, cols], in0=t[n, i][:], scalar=1.0, in1=partial[n - 1][:, cols],
                    op0=ADD, op1=MULT,
                )

        with tc.manual_schedule():
            for s in range(RAWS):
                load_u(s)
            multiplied = combined = 0
            for s in range(U_PASSES + LAG):
                if s < U_PASSES:
                    regroup(s)
                    if s % 2 == 1 and s + RAWS < U_PASSES:
                        load_u(s + RAWS - 1)
                        load_u(s + RAWS)
                beside = 2 * (s - Z_STEP)
                if 0 <= beside < len(z_work):
                    for work in z_work[beside]:
                        work()
                if s >= LAG:
                    quantise(s - LAG)
                if 0 <= beside < len(z_work) - 1:
                    for work in z_work[beside + 1]:
                        work()
                if s > z_done:
                    for i in range(CATCH_UP):
                        if multiplied <= s - LAG:
                            multiply(multiplied)
                            multiplied += 1
                    if combined < FACTORS - 1 and multiplied >= (combined + 1) * PIXEL_PASSES + CATCH_UP:
                        combine(combined)
                        combined += 1
            for n in range(combined, FACTORS):
                while multiplied < (n + 1) * PIXEL_PASSES:
                    multiply(multiplied)
                    multiplied += 1
                combine(n)

            for r in range(4):
                nc.sync.dma_start(
                    out=c_scales[r : P : 32, :].bitcast(I32), in_=C_scales[0, r : 16 : 4, :].bitcast(I32)
                )
            c_words_hbm = C_words[0].rearrange("p n t -> p (n t)").bitcast(I32)
            for i in range(LAST_PIECES):
                part = slice(i * PIXELS // LAST_PIECES, (i + 1) * PIXELS // LAST_PIECES)
                nc.sync.dma_start(out=c_words[:, part].bitcast(I32), in_=c_words_hbm[:, part])
                nc.sync.dma_start(out=beta_all[:, part], in_=beta[part].partition_broadcast(P))

            h_sb = partial[FACTORS - 1]
            hT = psum.tile([P, 2, P], F32, name="hT", tag="bank")
            transpose_words(nc, hT[:], h_sb[:], 0, ident[:])
            h_grouped = keep.tile([P, P, PACK], BF16, align_bytes=64)
            nc.scalar.copy(out=h_grouped[:].bitcast(F32), in_=hT[:].rearrange("p u b -> p b u"))
            h_codes = keep.tile([P, P], U32, align_bytes=64)
            h_scales = keep.tile([P, P], U8, align_bytes=64)
            nc.vector.quantize_mx(
                out=h_codes[:].bitcast(FP8X4),
                scales=h_scales[:],
                in_=h_grouped[:].rearrange("p b j -> p (b j)"),
            )

            for o in range(OUT_BANKS):
                hw = psum.tile([P, BANK], F32, name="hw", tag="bank")
                result = result_pool.tile([P, BANK], F32, name="result")
                cols = slice(o * BANK, (o + 1) * BANK)
                nc.tensor.matmul_mx(
                    out=hw[:],
                    lhsT=h_codes[:].bitcast(FP8X4),
                    lhsT_scale=h_scales[:],
                    rhs=c_words[:, cols].bitcast(FP8X4),
                    rhs_scale=c_scales[:, cols],
                    start=True,
                    stop=True,
                )
                nc.vector.tensor_add(out=result[:], in0=hw[:], in1=beta_all[:, cols])
                nc.sync.dma_start(out=out_rows[:, cols], in_=result[:])
